import numpy as np
import ml_dtypes


def mxq(x, axis, fmt="e4m3"):
    dtype, down = {"e4m3": (ml_dtypes.float8_e4m3fn, 7), "e5m2": (ml_dtypes.float8_e5m2, 14)}[fmt]
    v = np.moveaxis(np.asarray(x, np.float32).astype(ml_dtypes.bfloat16).astype(np.float64), axis, -1)
    blocks = v.reshape(v.shape[:-1] + (-1, 32))
    amax = np.abs(blocks).max(-1, keepdims=True)
    byte = np.maximum(np.where(amax > 0, np.frexp(amax)[1] - 1 + 127, 0) - down, 1)
    scale = np.exp2(byte - 127.0)
    codes = (blocks / scale).astype(np.float32).astype(dtype).astype(np.float64)
    return np.moveaxis((codes * scale).reshape(v.shape), -1, axis)


WIDE = False


def mx_kscale(k):
    if not WIDE:
        return np.ones(k)
    levels = np.array([10, -10, 5, -5, 0])
    a = np.random.permutation(np.resize(levels, k // 512 * 4)).reshape(k // 512, 4)
    idx = np.arange(k)
    return np.exp2(a[idx // 512, idx % 128 // 32])


BF16 = ml_dtypes.bfloat16


def bf(x):
    return np.asarray(x, np.float32).astype(BF16)


def f64(x):
    return np.asarray(x).astype(np.float64)


B, D_IN, D_H, D_OUT, SIZE_N, SIZE_M = 8192, 1024, 512, 256, 1024, 256
N_W1 = D_H * D_IN
N_B1 = D_H
N_W2 = D_OUT * D_H
N_B2 = D_OUT


def setup_inputs():
    s = mx_kscale(D_IN)
    r = s.min() / s
    bound = np.sqrt(12.0) / 2.0 * SIZE_M ** (-0.25)
    return {"x": bf(np.random.standard_normal((B, D_IN)) * s),
            "V1": bf(np.random.uniform(-bound, bound, (SIZE_N, SIZE_M))),
            "V2": bf(np.random.uniform(-bound, bound, (SIZE_M, SIZE_N)) * np.tile(r, SIZE_N // D_IN)),
            "w1_p": bf((1.0 + 0.1 * np.random.standard_normal(1)) / np.sqrt(D_IN) / s.min()),
            "b1_p": bf(0.5 * (1.0 + 0.1 * np.random.standard_normal(1))),
            "w2_p": bf(1.4 * (1.0 + 0.1 * np.random.standard_normal(1)) / np.sqrt(D_H)),
            "b2_p": bf(0.5 * (1.0 + 0.1 * np.random.standard_normal(1)))}


def reference(x, V1, V2, w1_p, b1_p, w2_p, b2_p):
    vflat = (f64(V1) @ f64(V2)).reshape(-1)
    o = 0
    w1 = (f64(w1_p)[0] * vflat[o:o + N_W1]).reshape(D_H, D_IN)
    o += N_W1
    b1 = (f64(b1_p)[0] * vflat[o:o + N_B1]).reshape(D_H)
    o += N_B1
    w2 = (f64(w2_p)[0] * vflat[o:o + N_W2]).reshape(D_OUT, D_H)
    o += N_W2
    b2 = (f64(b2_p)[0] * vflat[o:o + N_B2]).reshape(D_OUT)
    h = np.maximum((mxq(f64(x), 1, "e4m3") @ mxq(w1, 1, "e4m3").T) + b1, 0.0)
    y = (mxq(h, 1, "e4m3") @ mxq(w2, 1, "e4m3").T) + b2
    return y

@@ -1,0 +1,251 @@
+from contextlib import ExitStack
+
+import concourse.mybir as mybir
+from concourse.masks import make_identity
+
+F32 = mybir.dt.float32
+BF16 = mybir.dt.bfloat16
+U32 = mybir.dt.uint32
+U8 = mybir.dt.uint8
+FP8X4 = mybir.dt.float8_e4m3fn_x4
+ACT = mybir.ActivationFunctionType
+ALU = mybir.AluOpType
+
+P = 128
+B, D_IN, D_H, D_OUT = 8192, 1024, 512, 256
+RANK = 256
+CH = 512
+NCH = B // CH
+FLOPS = 2 * B * D_IN * D_H + 2 * B * D_H * D_OUT + 2 * 1024 * RANK * 1024
+
+
+def tile_feathernet_t_kernel(tc, x, V1, V2, w1_p, b1_p, w2_p, b2_p, out):
+    nc = tc.nc
+    with ExitStack() as ctx:
+        ctx.enter_context(tc.manual_schedule())
+        const = ctx.enter_context(tc.tile_pool(name="const", bufs=1))
+        xin = ctx.enter_context(tc.tile_pool(name="xin", bufs=NCH))
+        work = ctx.enter_context(tc.tile_pool(name="work", bufs=2))
+        ypool = ctx.enter_context(tc.tile_pool(name="ypool", bufs=4))
+        psx = ctx.enter_context(tc.psum_pool(name="psx", bufs=3))
+        psh = ctx.enter_context(tc.psum_pool(name="psh", bufs=4))
+        psy = ctx.enter_context(tc.psum_pool(name="psy", bufs=1))
+
+        v1_sb = const.tile([P, 6, RANK], BF16)
+        nc.sync.dma_start(out=v1_sb[:, 0:5, :], in_=V1[0:640, :].rearrange("(a p) m -> p a m", p=P))
+        nc.sync.dma_start(out=v1_sb[:, 5, :], in_=V1[513:641, :])
+        v2_sb = const.tile([P, 2, 1024], BF16)
+        nc.sync.dma_start(out=v2_sb[:], in_=V2.rearrange("(c p) n -> p c n", p=P))
+        gains_bf = []
+        with nc.allow_non_contiguous_dma(reason="one bfloat16 gain to every partition"):
+            for i, gain in enumerate((w1_p, b1_p, w2_p, b2_p)):
+                gb = const.tile([P, 1], BF16, name="gain_bf%d" % i)
+                nc.scalar.dma_start(out=gb[:], in_=gain.partition_broadcast(P))
+                gains_bf.append(gb)
+        x_sb = []
+        for c in range(NCH):
+            xt_in = xin.tile([P, 4 * D_IN], BF16, name="x_sb")
+            nc.sync.dma_start(
+                out=xt_in[:],
+                in_=x[c * CH:(c + 1) * CH, :].rearrange("(p s) k -> p (s k)", s=4),
+            )
+            x_sb.append(xt_in)
+
+        ident_bf = const.tile([P, P], BF16)
+        make_identity(nc, ident_bf[:])
+        ident_f = const.tile([P, P], F32)
+        make_identity(nc, ident_f[:])
+
+        g32 = const.tile([P, 4], F32)
+        for i in range(4):
+            nc.vector.tensor_copy(out=g32[:, i:i + 1], in_=gains_bf[i][:])
+
+        v1T = const.tile([P, 2, 6 * P], BF16)
+        for mc in range(2):
+            tp = psx.tile([P, 4, P], BF16, tag="xt", name="tp")
+            for a in range(4):
+                nc.tensor.transpose(tp[:, a, :], v1_sb[:, a, mc * P:(mc + 1) * P], ident_bf[:])
+            if mc == 0:
+                nc.vector.tensor_copy(out=v1T[:, mc, 0:512], in_=tp[:].rearrange("p a r -> p (a r)"))
+            else:
+                nc.scalar.copy(out=v1T[:, mc, 0:512], in_=tp[:].rearrange("p a r -> p (a r)"))
+        tp2 = psx.tile([P, 2, 2 * P], BF16, tag="xt", name="tp2")
+        for mc in range(2):
+            for a in range(2):
+                nc.tensor.transpose(tp2[:, mc, a * P:(a + 1) * P], v1_sb[:, 4 + a, mc * P:(mc + 1) * P], ident_bf[:])
+        nc.vector.tensor_copy(out=v1T[:, :, 512:768], in_=tp2[:])
+
+        v2_k = v2_sb[:].rearrange("p c (b q e) -> p c b e q", b=4, e=2)
+        w1g = const.tile([P, 2, D_H, 4], BF16, align_bytes=64)
+        w1c = const.tile([P, 2 * D_H], U32, align_bytes=64)
+        w1s = const.tile([P, 2 * D_H], U8, align_bytes=64)
+        for g in range(2):
+            for rc in range(4):
+                wp = psh.tile([P, 4, P], F32, tag="h", name="wp")
+                for j in range(4):
+                    u, e = j // 2, j % 2
+                    for mc in range(2):
+                        nc.tensor.matmul(
+                            wp[:, j, :],
+                            lhsT=v2_k[:, mc, 2 * g + u, e, :],
+                            rhs=v1T[:, mc, rc * P:(rc + 1) * P],
+                            start=(mc == 0),
+                            stop=(mc == 1),
+                        )
+                dst = w1g[:, g, rc * P:(rc + 1) * P, :]
+                src = wp[:].rearrange("p j r -> p r j")
+                if rc % 2 == 0:
+                    nc.scalar.activation(out=dst, in_=src, func=ACT.Copy, scale=g32[:, 0:1])
+                else:
+                    nc.vector.tensor_scalar(out=dst, in0=src, scalar1=g32[:, 0:1], scalar2=None, op0=ALU.mult)
+            nc.vector.quantize_mx(
+                out=w1c[:, g * D_H:(g + 1) * D_H].bitcast(FP8X4),
+                scales=w1s[:, g * D_H:(g + 1) * D_H],
+                in_=w1g[:, g, :, :].rearrange("p r j -> p (r j)"),
+            )
+
+        bp = psy.tile([P, 4, 32], F32, tag="y", name="bp")
+        for t in range(4):
+            for mc in range(2):
+                nc.tensor.matmul(
+                    bp[:, t, :],
+                    lhsT=v2_sb[:, mc, t * P:(t + 1) * P],
+                    rhs=v1T[:, mc, 512:544],
+                    start=(mc == 0),
+                    stop=(mc == 1),
+                )
+        b1_sb = const.tile([P, 4], F32)
+        nc.vector.tensor_scalar(out=b1_sb[:], in0=bp[:, :, 0], scalar1=g32[:, 1:2], scalar2=None, op0=ALU.mult)
+
+        w2g = const.tile([P, P, 2, 4], BF16, align_bytes=64)
+        w2c = const.tile([P, D_OUT], U32, align_bytes=64)
+        w2s = const.tile([P, D_OUT], U8, align_bytes=64)
+        for par in range(2):
+            wq = psx.tile([P, 4, P], F32, tag="xt", name="wq")
+            for t in range(4):
+                col = t * P + (512 if par == 0 else 0)
+                row = 512 if par == 0 else 640
+                for mc in range(2):
+                    nc.tensor.matmul(
+                        wq[:, t, :],
+                        lhsT=v2_sb[:, mc, col:col + P],
+                        rhs=v1T[:, mc, row:row + P],
+                        start=(mc == 0),
+                        stop=(mc == 1),
+                    )
+            nc.scalar.activation(
+                out=w2g[:, :, par, :], in_=wq[:].rearrange("p t a -> p a t"), func=ACT.Copy, scale=g32[:, 2:3]
+            )
+        nc.vector.quantize_mx(
+            out=w2c[:].bitcast(FP8X4), scales=w2s[:], in_=w2g[:].rearrange("p a q t -> p (a q t)")
+        )
+
+        b2p = psy.tile([P, D_OUT], F32, tag="y", name="b2p")
+        for mc in range(2):
+            nc.tensor.matmul(
+                b2p[:],
+                lhsT=v1T[:, mc, 767:768].to_broadcast([P, P]),
+                rhs=v2_sb[:, mc, 512:768],
+                start=(mc == 0),
+                stop=(mc == 1),
+            )
+        b2bc = const.tile([P, 2, D_OUT], F32)
+        for i in range(2):
+            nc.scalar.activation(out=b2bc[:, i, :], in_=b2p[:], func=ACT.Copy, scale=g32[:, 3:4])
+
+        xg, xc, xs, hb, hg, hc, hs, ysb = {}, {}, {}, {}, {}, {}, {}, {}
+
+        def transposes(c):
+            xw = x_sb[c][:].bitcast(F32).rearrange("p (s w) -> p s w", s=4)
+            xg[c] = work.tile([P, 4 * D_IN], BF16, align_bytes=64, name="xg")
+            xgf = xg[c][:].bitcast(F32).rearrange("p (g n u) -> p g n u", g=2, u=2)
+            for g in range(2):
+                for sp in range(2):
+                    xt = psx.tile([P, 2, 2 * P], F32, tag="xt", name="xt")
+                    for s2 in range(2):
+                        for u in range(2):
+                            w0 = 256 * g + 128 * u
+                            nc.tensor.transpose(
+                                xt[:, u, s2 * P:(s2 + 1) * P], xw[:, 2 * sp + s2, w0:w0 + P], ident_f[:]
+                            )
+                    nc.scalar.copy(
+                        out=xgf[:, g, 256 * sp:256 * (sp + 1), :], in_=xt[:].rearrange("p u n -> p n u")
+                    )
+
+        def quant_x(c):
+            xc[c] = work.tile([P, 2 * CH], U32, align_bytes=64, name="xc")
+            xs[c] = work.tile([P, 2 * CH], U8, align_bytes=64, name="xs")
+            for g in range(2):
+                nc.vector.quantize_mx(
+                    out=xc[c][:, g * CH:(g + 1) * CH].bitcast(FP8X4),
+                    scales=xs[c][:, g * CH:(g + 1) * CH],
+                    in_=xg[c][:, g * 4 * CH:(g + 1) * 4 * CH],
+                )
+
+        def layer1(c):
+            hb[c] = work.tile([P, 4, CH], BF16, name="hb")
+            for t in range(4):
+                hp = psh.tile([P, CH], F32, tag="h", name="hp")
+                for g in range(2):
+                    k0 = g * D_H + t * P
+                    nc.tensor.matmul_mx(
+                        out=hp[:],
+                        lhsT=w1c[:, k0:k0 + P].bitcast(FP8X4),
+                        lhsT_scale=w1s[:, k0:k0 + P],
+                        rhs=xc[c][:, g * CH:(g + 1) * CH].bitcast(FP8X4),
+                        rhs_scale=xs[c][:, g * CH:(g + 1) * CH],
+                        start=(g == 0),
+                        stop=(g == 1),
+                    )
+                nc.scalar.activation(out=hb[c][:, t, :], in_=hp[:], func=ACT.Relu, bias=b1_sb[:, t:t + 1], scale=1.0)
+
+        def regroup_h(c):
+            hg[c] = work.tile([P, CH, 4], BF16, align_bytes=64, name="hg")
+            nc.vector.tensor_copy(
+                out=hg[c][:].rearrange("p (c i) t -> p c t i", i=4),
+                in_=hb[c][:].rearrange("p t (c i) -> p c t i", i=4),
+            )
+
+        def quant_h(c):
+            hc[c] = work.tile([P, CH], U32, align_bytes=64, name="hc")
+            hs[c] = work.tile([P, CH], U8, align_bytes=64, name="hs")
+            nc.vector.quantize_mx(
+                out=hc[c][:].bitcast(FP8X4), scales=hs[c][:], in_=hg[c][:].rearrange("p n t -> p (n t)")
+            )
+
+        def layer2(c, half):
+            if half == 0:
+                ysb[c] = ypool.tile([P, 4, D_OUT], F32, name="ysb")
+            yp = psy.tile([P, 2, D_OUT], F32, tag="y", name="yp")
+            for s2 in range(2):
+                s = 2 * half + s2
+                nc.tensor.matmul_mx(
+                    out=yp[:, s2, :],
+                    lhsT=hc[c][:, s * P:(s + 1) * P].bitcast(FP8X4),
+                    lhsT_scale=hs[c][:, s * P:(s + 1) * P],
+                    rhs=w2c[:].bitcast(FP8X4),
+                    rhs_scale=w2s[:],
+                    start=True,
+                    stop=True,
+                )
+            nc.vector.tensor_tensor(out=ysb[c][:, 2 * half:2 * half + 2, :], in0=yp[:], in1=b2bc[:], op=ALU.add)
+            if half == 1:
+                nc.sync.dma_start(
+                    out=out[c * CH:(c + 1) * CH, :].rearrange("(p s) o -> p s o", s=4), in_=ysb[c][:]
+                )
+
+        for c in range(-1, NCH + 2):
+            if 0 <= c + 1 < NCH:
+                transposes(c + 1)
+            if 0 <= c - 1 < NCH:
+                regroup_h(c - 1)
+            if 0 <= c - 2 < NCH:
+                layer2(c - 2, 1)
+            if 0 <= c - 1 < NCH:
+                quant_h(c - 1)
+            if 0 <= c + 1 < NCH:
+                quant_x(c + 1)
+            if 0 <= c < NCH:
+                layer1(c)
+            if 0 <= c - 1 < NCH:
+                layer2(c - 1, 0)

@@ -16,6 +16,8 @@ B, D_IN, D_H, D_OUT = 8192, 1024, 512, 256
 RANK = 256
 CH = 512
 NCH = B // CH
+LEAD = 2
+G_TOK = 256
 FLOPS = 2 * B * D_IN * D_H + 2 * B * D_H * D_OUT + 2 * 1024 * RANK * 1024
 
 
@@ -27,9 +29,8 @@ def tile_feathernet_t_kernel(tc, x, V1, V2, w1_p, b1_p, w2_p, b2_p, out):
         xin = ctx.enter_context(tc.tile_pool(name="xin", bufs=NCH))
         work = ctx.enter_context(tc.tile_pool(name="work", bufs=2))
         ypool = ctx.enter_context(tc.tile_pool(name="ypool", bufs=4))
-        psx = ctx.enter_context(tc.psum_pool(name="psx", bufs=3))
-        psh = ctx.enter_context(tc.psum_pool(name="psh", bufs=4))
-        psy = ctx.enter_context(tc.psum_pool(name="psy", bufs=1))
+        xq = ctx.enter_context(tc.tile_pool(name="xq", bufs=LEAD + 1))
+        psum = ctx.enter_context(tc.psum_pool(name="psum", bufs=8))
 
         v1_sb = const.tile([P, 6, RANK], BF16)
         nc.sync.dma_start(out=v1_sb[:, 0:5, :], in_=V1[0:640, :].rearrange("(a p) m -> p a m", p=P))
@@ -62,14 +63,14 @@ def tile_feathernet_t_kernel(tc, x, V1, V2, w1_p, b1_p, w2_p, b2_p, out):
 
         v1T = const.tile([P, 2, 6 * P], BF16)
         for mc in range(2):
-            tp = psx.tile([P, 4, P], BF16, tag="xt", name="tp")
+            tp = psum.tile([P, 4, P], BF16, tag="ps", name="tp")
             for a in range(4):
                 nc.tensor.transpose(tp[:, a, :], v1_sb[:, a, mc * P:(mc + 1) * P], ident_bf[:])
             if mc == 0:
                 nc.vector.tensor_copy(out=v1T[:, mc, 0:512], in_=tp[:].rearrange("p a r -> p (a r)"))
             else:
                 nc.scalar.copy(out=v1T[:, mc, 0:512], in_=tp[:].rearrange("p a r -> p (a r)"))
-        tp2 = psx.tile([P, 2, 2 * P], BF16, tag="xt", name="tp2")
+        tp2 = psum.tile([P, 2, 2 * P], BF16, tag="ps", name="tp2")
         for mc in range(2):
             for a in range(2):
                 nc.tensor.transpose(tp2[:, mc, a * P:(a + 1) * P], v1_sb[:, 4 + a, mc * P:(mc + 1) * P], ident_bf[:])
@@ -81,7 +82,7 @@ def tile_feathernet_t_kernel(tc, x, V1, V2, w1_p, b1_p, w2_p, b2_p, out):
         w1s = const.tile([P, 2 * D_H], U8, align_bytes=64)
         for g in range(2):
             for rc in range(4):
-                wp = psh.tile([P, 4, P], F32, tag="h", name="wp")
+                wp = psum.tile([P, 4, P], F32, tag="ps", name="wp")
                 for j in range(4):
                     u, e = j // 2, j % 2
                     for mc in range(2):
@@ -104,7 +105,7 @@ def tile_feathernet_t_kernel(tc, x, V1, V2, w1_p, b1_p, w2_p, b2_p, out):
                 in_=w1g[:, g, :, :].rearrange("p r j -> p (r j)"),
             )
 
-        bp = psy.tile([P, 4, 32], F32, tag="y", name="bp")
+        bp = psum.tile([P, 4, 32], F32, tag="ps", name="bp")
         for t in range(4):
             for mc in range(2):
                 nc.tensor.matmul(
@@ -121,7 +122,7 @@ def tile_feathernet_t_kernel(tc, x, V1, V2, w1_p, b1_p, w2_p, b2_p, out):
         w2c = const.tile([P, D_OUT], U32, align_bytes=64)
         w2s = const.tile([P, D_OUT], U8, align_bytes=64)
         for par in range(2):
-            wq = psx.tile([P, 4, P], F32, tag="xt", name="wq")
+            wq = psum.tile([P, 4, P], F32, tag="ps", name="wq")
             for t in range(4):
                 col = t * P + (512 if par == 0 else 0)
                 row = 512 if par == 0 else 640
@@ -140,7 +141,7 @@ def tile_feathernet_t_kernel(tc, x, V1, V2, w1_p, b1_p, w2_p, b2_p, out):
             out=w2c[:].bitcast(FP8X4), scales=w2s[:], in_=w2g[:].rearrange("p a q t -> p (a q t)")
         )
 
-        b2p = psy.tile([P, D_OUT], F32, tag="y", name="b2p")
+        b2p = psum.tile([P, D_OUT], F32, tag="ps", name="b2p")
         for mc in range(2):
             nc.tensor.matmul(
                 b2p[:],
@@ -161,20 +162,23 @@ def tile_feathernet_t_kernel(tc, x, V1, V2, w1_p, b1_p, w2_p, b2_p, out):
             xgf = xg[c][:].bitcast(F32).rearrange("p (g n u) -> p g n u", g=2, u=2)
             for g in range(2):
                 for sp in range(2):
-                    xt = psx.tile([P, 2, 2 * P], F32, tag="xt", name="xt")
+                    xt = psum.tile([P, 2, 2 * P], F32, tag="ps", name="xt")
                     for s2 in range(2):
                         for u in range(2):
                             w0 = 256 * g + 128 * u
                             nc.tensor.transpose(
                                 xt[:, u, s2 * P:(s2 + 1) * P], xw[:, 2 * sp + s2, w0:w0 + P], ident_f[:]
                             )
-                    nc.scalar.copy(
-                        out=xgf[:, g, 256 * sp:256 * (sp + 1), :], in_=xt[:].rearrange("p u n -> p n u")
-                    )
+                    dst = xgf[:, g, 256 * sp:256 * (sp + 1), :]
+                    src = xt[:].rearrange("p u n -> p n u")
+                    if c <= LEAD and sp == 1:
+                        nc.vector.tensor_copy(out=dst, in_=src)
+                    else:
+                        nc.scalar.copy(out=dst, in_=src)
 
         def quant_x(c):
-            xc[c] = work.tile([P, 2 * CH], U32, align_bytes=64, name="xc")
-            xs[c] = work.tile([P, 2 * CH], U8, align_bytes=64, name="xs")
+            xc[c] = xq.tile([P, 2 * CH], U32, align_bytes=64, name="xc")
+            xs[c] = xq.tile([P, 2 * CH], U8, align_bytes=64, name="xs")
             for g in range(2):
                 nc.vector.quantize_mx(
                     out=xc[c][:, g * CH:(g + 1) * CH].bitcast(FP8X4),
@@ -185,7 +189,7 @@ def tile_feathernet_t_kernel(tc, x, V1, V2, w1_p, b1_p, w2_p, b2_p, out):
         def layer1(c):
             hb[c] = work.tile([P, 4, CH], BF16, name="hb")
             for t in range(4):
-                hp = psh.tile([P, CH], F32, tag="h", name="hp")
+                hp = psum.tile([P, CH], F32, tag="ps", name="hp")
                 for g in range(2):
                     k0 = g * D_H + t * P
                     nc.tensor.matmul_mx(
@@ -197,55 +201,73 @@ def tile_feathernet_t_kernel(tc, x, V1, V2, w1_p, b1_p, w2_p, b2_p, out):
                         start=(g == 0),
                         stop=(g == 1),
                     )
-                nc.scalar.activation(out=hb[c][:, t, :], in_=hp[:], func=ACT.Relu, bias=b1_sb[:, t:t + 1], scale=1.0)
+                if t == 3:
+                    nc.vector.tensor_scalar(
+                        out=hb[c][:, t, :], in0=hp[:], scalar1=b1_sb[:, t:t + 1], scalar2=0.0, op0=ALU.add, op1=ALU.max
+                    )
+                else:
+                    nc.scalar.activation(
+                        out=hb[c][:, t, :], in_=hp[:], func=ACT.Relu, bias=b1_sb[:, t:t + 1], scale=1.0
+                    )
 
         def regroup_h(c):
             hg[c] = work.tile([P, CH, 4], BF16, align_bytes=64, name="hg")
+            v_tok = CH - G_TOK
+            if G_TOK > 0:
+                nc.gpsimd.tensor_scalar(
+                    out=hg[c][:, v_tok:CH, :],
+                    in0=hb[c][:, :, v_tok:CH].rearrange("p t n -> p n t"),
+                    scalar1=1.0,
+                    scalar2=0.0,
+                    op0=ALU.mult,
+                    op1=ALU.add,
+                )
             nc.vector.tensor_copy(
-                out=hg[c][:].rearrange("p (c i) t -> p c t i", i=4),
-                in_=hb[c][:].rearrange("p t (c i) -> p c t i", i=4),
+                out=hg[c][:, 0:v_tok, :].rearrange("p (c i) t -> p c t i", i=4),
+                in_=hb[c][:, :, 0:v_tok].rearrange("p t (c i) -> p c t i", i=4),
             )
 
         def quant_h(c):
             hc[c] = work.tile([P, CH], U32, align_bytes=64, name="hc")
             hs[c] = work.tile([P, CH], U8, align_bytes=64, name="hs")
-            nc.vector.quantize_mx(
-                out=hc[c][:].bitcast(FP8X4), scales=hs[c][:], in_=hg[c][:].rearrange("p n t -> p (n t)")
-            )
-
-        def layer2(c, half):
-            if half == 0:
-                ysb[c] = ypool.tile([P, 4, D_OUT], F32, name="ysb")
-            yp = psy.tile([P, 2, D_OUT], F32, tag="y", name="yp")
-            for s2 in range(2):
-                s = 2 * half + s2
-                nc.tensor.matmul_mx(
-                    out=yp[:, s2, :],
-                    lhsT=hc[c][:, s * P:(s + 1) * P].bitcast(FP8X4),
-                    lhsT_scale=hs[c][:, s * P:(s + 1) * P],
-                    rhs=w2c[:].bitcast(FP8X4),
-                    rhs_scale=w2s[:],
-                    start=True,
-                    stop=True,
-                )
-            nc.vector.tensor_tensor(out=ysb[c][:, 2 * half:2 * half + 2, :], in0=yp[:], in1=b2bc[:], op=ALU.add)
-            if half == 1:
-                nc.sync.dma_start(
-                    out=out[c * CH:(c + 1) * CH, :].rearrange("(p s) o -> p s o", s=4), in_=ysb[c][:]
+            for half in range(2):
+                n0 = half * 256
+                nc.vector.quantize_mx(
+                    out=hc[c][:, n0:n0 + 256].bitcast(FP8X4),
+                    scales=hs[c][:, n0:n0 + 256],
+                    in_=hg[c][:, n0:n0 + 256, :].rearrange("p n t -> p (n t)"),
                 )
 
-        for c in range(-1, NCH + 2):
-            if 0 <= c + 1 < NCH:
-                transposes(c + 1)
-            if 0 <= c - 1 < NCH:
+        def layer2(c):
+            ysb[c] = ypool.tile([P, 4, D_OUT], F32, name="ysb")
+            for half in range(2):
+                yp = psum.tile([P, 2, D_OUT], F32, tag="ps", name="yp")
+                for s2 in range(2):
+                    s = 2 * half + s2
+                    nc.tensor.matmul_mx(
+                        out=yp[:, s2, :],
+                        lhsT=hc[c][:, s * P:(s + 1) * P].bitcast(FP8X4),
+                        lhsT_scale=hs[c][:, s * P:(s + 1) * P],
+                        rhs=w2c[:].bitcast(FP8X4),
+                        rhs_scale=w2s[:],
+                        start=True,
+                        stop=True,
+                    )
+                nc.vector.tensor_tensor(out=ysb[c][:, 2 * half:2 * half + 2, :], in0=yp[:], in1=b2bc[:], op=ALU.add)
+            nc.sync.dma_start(out=out[c * CH:(c + 1) * CH, :].rearrange("(p s) o -> p s o", s=4), in_=ysb[c][:])
+
+        for c in range(LEAD):
+            transposes(c)
+            quant_x(c)
+        for c in range(NCH + 1):
+            if c + LEAD < NCH:
+                transposes(c + LEAD)
+            if c >= 1:
                 regroup_h(c - 1)
-            if 0 <= c - 2 < NCH:
-                layer2(c - 2, 1)
-            if 0 <= c - 1 < NCH:
                 quant_h(c - 1)
-            if 0 <= c + 1 < NCH:
-                quant_x(c + 1)
-            if 0 <= c < NCH:
+            if c + LEAD < NCH:
+                quant_x(c + LEAD)
+            if c < NCH:
                 layer1(c)
-            if 0 <= c - 1 < NCH:
-                layer2(c - 1, 0)
+            if c >= 1:
+                layer2(c - 1)

@@ -156,11 +156,12 @@ def tile_feathernet_t_kernel(tc, x, V1, V2, w1_p, b1_p, w2_p, b2_p, out):
 
         xg, xc, xs, hb, hg, hc, hs, ysb = {}, {}, {}, {}, {}, {}, {}, {}
 
-        def transposes(c):
+        def transposes(c, g):
             xw = x_sb[c][:].bitcast(F32).rearrange("p (s w) -> p s w", s=4)
-            xg[c] = work.tile([P, 4 * D_IN], BF16, align_bytes=64, name="xg")
+            if g == 0:
+                xg[c] = work.tile([P, 4 * D_IN], BF16, align_bytes=64, name="xg")
             xgf = xg[c][:].bitcast(F32).rearrange("p (g n u) -> p g n u", g=2, u=2)
-            for g in range(2):
+            if True:
                 for sp in range(2):
                     xt = psum.tile([P, 2, 2 * P], F32, tag="ps", name="xt")
                     for s2 in range(2):
@@ -186,9 +187,10 @@ def tile_feathernet_t_kernel(tc, x, V1, V2, w1_p, b1_p, w2_p, b2_p, out):
                     in_=xg[c][:, g * 4 * CH:(g + 1) * 4 * CH],
                 )
 
-        def layer1(c):
-            hb[c] = work.tile([P, 4, CH], BF16, name="hb")
-            for t in range(4):
+        def layer1(c, th):
+            if th == 0:
+                hb[c] = work.tile([P, 4, CH], BF16, name="hb")
+            for t in (2 * th, 2 * th + 1):
                 hp = psum.tile([P, CH], F32, tag="ps", name="hp")
                 for g in range(2):
                     k0 = g * D_H + t * P
@@ -257,17 +259,21 @@ def tile_feathernet_t_kernel(tc, x, V1, V2, w1_p, b1_p, w2_p, b2_p, out):
             nc.sync.dma_start(out=out[c * CH:(c + 1) * CH, :].rearrange("(p s) o -> p s o", s=4), in_=ysb[c][:])
 
         for c in range(LEAD):
-            transposes(c)
+            transposes(c, 0)
+            transposes(c, 1)
             quant_x(c)
         for c in range(NCH + 1):
             if c + LEAD < NCH:
-                transposes(c + LEAD)
+                transposes(c + LEAD, 0)
             if c >= 1:
                 regroup_h(c - 1)
                 quant_h(c - 1)
+            if c < NCH:
+                layer1(c, 0)
             if c + LEAD < NCH:
+                transposes(c + LEAD, 1)
                 quant_x(c + LEAD)
             if c < NCH:
-                layer1(c)
+                layer1(c, 1)
             if c >= 1:
                 layer2(c - 1)

@@ -17,6 +17,7 @@ RANK = 256
 CH = 512
 NCH = B // CH
 LEAD = 2
+V_H_BANK = -1
 G_TOK = 256
 FLOPS = 2 * B * D_IN * D_H + 2 * B * D_H * D_OUT + 2 * 1024 * RANK * 1024
 
@@ -156,12 +157,11 @@ def tile_feathernet_t_kernel(tc, x, V1, V2, w1_p, b1_p, w2_p, b2_p, out):
 
         xg, xc, xs, hb, hg, hc, hs, ysb = {}, {}, {}, {}, {}, {}, {}, {}
 
-        def transposes(c, g):
+        def transposes(c):
             xw = x_sb[c][:].bitcast(F32).rearrange("p (s w) -> p s w", s=4)
-            if g == 0:
-                xg[c] = work.tile([P, 4 * D_IN], BF16, align_bytes=64, name="xg")
+            xg[c] = work.tile([P, 4 * D_IN], BF16, align_bytes=64, name="xg")
             xgf = xg[c][:].bitcast(F32).rearrange("p (g n u) -> p g n u", g=2, u=2)
-            if True:
+            for g in range(2):
                 for sp in range(2):
                     xt = psum.tile([P, 2, 2 * P], F32, tag="ps", name="xt")
                     for s2 in range(2):
@@ -187,10 +187,9 @@ def tile_feathernet_t_kernel(tc, x, V1, V2, w1_p, b1_p, w2_p, b2_p, out):
                     in_=xg[c][:, g * 4 * CH:(g + 1) * 4 * CH],
                 )
 
-        def layer1(c, th):
-            if th == 0:
-                hb[c] = work.tile([P, 4, CH], BF16, name="hb")
-            for t in (2 * th, 2 * th + 1):
+        def layer1(c):
+            hb[c] = work.tile([P, 4, CH], BF16, name="hb")
+            for t in range(4):
                 hp = psum.tile([P, CH], F32, tag="ps", name="hp")
                 for g in range(2):
                     k0 = g * D_H + t * P
@@ -203,7 +202,7 @@ def tile_feathernet_t_kernel(tc, x, V1, V2, w1_p, b1_p, w2_p, b2_p, out):
                         start=(g == 0),
                         stop=(g == 1),
                     )
-                if t == 3:
+                if t == V_H_BANK:
                     nc.vector.tensor_scalar(
                         out=hb[c][:, t, :], in0=hp[:], scalar1=b1_sb[:, t:t + 1], scalar2=0.0, op0=ALU.add, op1=ALU.max
                     )
@@ -259,21 +258,17 @@ def tile_feathernet_t_kernel(tc, x, V1, V2, w1_p, b1_p, w2_p, b2_p, out):
             nc.sync.dma_start(out=out[c * CH:(c + 1) * CH, :].rearrange("(p s) o -> p s o", s=4), in_=ysb[c][:])
 
         for c in range(LEAD):
-            transposes(c, 0)
-            transposes(c, 1)
+            transposes(c)
             quant_x(c)
         for c in range(NCH + 1):
             if c + LEAD < NCH:
-                transposes(c + LEAD, 0)
+                transposes(c + LEAD)
             if c >= 1:
                 regroup_h(c - 1)
                 quant_h(c - 1)
-            if c < NCH:
-                layer1(c, 0)
             if c + LEAD < NCH:
-                transposes(c + LEAD, 1)
                 quant_x(c + LEAD)
             if c < NCH:
-                layer1(c, 1)
+                layer1(c)
             if c >= 1:
                 layer2(c - 1)

@@ -15,10 +15,12 @@ P = 128
 B, D_IN, D_H, D_OUT = 8192, 1024, 512, 256
 RANK = 256
 CH = 512
+HALF = CH // 2
 NCH = B // CH
 LEAD = 2
-V_H_BANK = -1
-G_TOK = 256
+LAG = 2
+X_ON_V = (1, 0, 0)
+WARM_A, WARM_B = 4, 2
 FLOPS = 2 * B * D_IN * D_H + 2 * B * D_H * D_OUT + 2 * 1024 * RANK * 1024
 
 
@@ -29,21 +31,26 @@ def tile_feathernet_t_kernel(tc, x, V1, V2, w1_p, b1_p, w2_p, b2_p, out):
         const = ctx.enter_context(tc.tile_pool(name="const", bufs=1))
         xin = ctx.enter_context(tc.tile_pool(name="xin", bufs=NCH))
         work = ctx.enter_context(tc.tile_pool(name="work", bufs=2))
-        ypool = ctx.enter_context(tc.tile_pool(name="ypool", bufs=4))
         xq = ctx.enter_context(tc.tile_pool(name="xq", bufs=LEAD + 1))
+        hq = ctx.enter_context(tc.tile_pool(name="hq", bufs=LAG + 1))
+        ypool = ctx.enter_context(tc.tile_pool(name="ypool", bufs=4))
         psum = ctx.enter_context(tc.psum_pool(name="psum", bufs=8))
 
+        ones = const.tile([P, CH], BF16)
+        nc.vector.memset(ones[:], 1.0)
+        gain_row = const.tile([P, 64], BF16)
+        nc.vector.memset(gain_row[:], 0.0)
+        ident_f = const.tile([P, P], F32)
+        make_identity(nc, ident_f[:])
+
         v1_sb = const.tile([P, 6, RANK], BF16)
-        nc.sync.dma_start(out=v1_sb[:, 0:5, :], in_=V1[0:640, :].rearrange("(a p) m -> p a m", p=P))
-        nc.sync.dma_start(out=v1_sb[:, 5, :], in_=V1[513:641, :])
         v2_sb = const.tile([P, 2, 1024], BF16)
-        nc.sync.dma_start(out=v2_sb[:], in_=V2.rearrange("(c p) n -> p c n", p=P))
-        gains_bf = []
-        with nc.allow_non_contiguous_dma(reason="one bfloat16 gain to every partition"):
-            for i, gain in enumerate((w1_p, b1_p, w2_p, b2_p)):
-                gb = const.tile([P, 1], BF16, name="gain_bf%d" % i)
-                nc.scalar.dma_start(out=gb[:], in_=gain.partition_broadcast(P))
-                gains_bf.append(gb)
+        nc.sync.dma_start(out=v1_sb[:, 0:4, :], in_=V1[0:512, :].rearrange("(a p) m -> p a m", p=P))
+        nc.sync.dma_start(out=v2_sb[:], in_=V2.rearrange("(q e) n -> q e n", e=2))
+        nc.sync.dma_start(out=v1_sb[:, 4, :], in_=V1[512:640, :])
+        nc.sync.dma_start(out=v1_sb[:, 5, :], in_=V1[513:641, :])
+        for i, gain in enumerate((w1_p, b1_p, w2_p, b2_p)):
+            nc.scalar.dma_start(out=gain_row[0:1, 16 * i:16 * i + 1], in_=gain.rearrange("(o n) -> o n", o=1))
         x_sb = []
         for c in range(NCH):
             xt_in = xin.tile([P, 4 * D_IN], BF16, name="x_sb")
@@ -53,29 +60,33 @@ def tile_feathernet_t_kernel(tc, x, V1, V2, w1_p, b1_p, w2_p, b2_p, out):
             )
             x_sb.append(xt_in)
 
-        ident_bf = const.tile([P, P], BF16)
-        make_identity(nc, ident_bf[:])
-        ident_f = const.tile([P, P], F32)
-        make_identity(nc, ident_f[:])
+        warm = psum.tile([P, CH], F32, tag="ps", name="warm")
 
-        g32 = const.tile([P, 4], F32)
-        for i in range(4):
-            nc.vector.tensor_copy(out=g32[:, i:i + 1], in_=gains_bf[i][:])
+        def dummies(n):
+            for i in range(n):
+                nc.tensor.matmul(warm[:], lhsT=ones[:, 0:P], rhs=ones[:], start=True, stop=True)
 
-        v1T = const.tile([P, 2, 6 * P], BF16)
-        for mc in range(2):
-            tp = psum.tile([P, 4, P], BF16, tag="ps", name="tp")
-            for a in range(4):
-                nc.tensor.transpose(tp[:, a, :], v1_sb[:, a, mc * P:(mc + 1) * P], ident_bf[:])
-            if mc == 0:
-                nc.vector.tensor_copy(out=v1T[:, mc, 0:512], in_=tp[:].rearrange("p a r -> p (a r)"))
-            else:
-                nc.scalar.copy(out=v1T[:, mc, 0:512], in_=tp[:].rearrange("p a r -> p (a r)"))
-        tp2 = psum.tile([P, 2, 2 * P], BF16, tag="ps", name="tp2")
-        for mc in range(2):
-            for a in range(2):
-                nc.tensor.transpose(tp2[:, mc, a * P:(a + 1) * P], v1_sb[:, 4 + a, mc * P:(mc + 1) * P], ident_bf[:])
-        nc.vector.tensor_copy(out=v1T[:, :, 512:768], in_=tp2[:])
+        dummies(WARM_A)
+
+        v1w = v1_sb[:].rearrange("p a m -> p (a m)").bitcast(F32)
+        v1T = const.tile([P, 6 * P], F32)
+        tpa = psum.tile([P, 4 * P], F32, tag="ps", name="tpa")
+        for a in range(4):
+            nc.tensor.transpose(tpa[:, a * P:(a + 1) * P], v1w[:, a * P:(a + 1) * P], ident_f[:])
+        nc.vector.tensor_copy(out=v1T[:, 0:4 * P], in_=tpa[:])
+        gp = psum.tile([P, 64], F32, tag="ps", name="gp")
+        nc.tensor.matmul(gp[:], lhsT=ones[:, 0:P], rhs=gain_row[:], start=True, stop=True)
+        g32 = const.tile([P, 64], F32)
+        nc.vector.tensor_copy(out=g32[:], in_=gp[:])
+        dummies(WARM_B)
+        tpb = psum.tile([P, 2 * P], F32, tag="ps", name="tpb")
+        for a in range(2):
+            nc.tensor.transpose(tpb[:, a * P:(a + 1) * P], v1w[:, (4 + a) * P:(5 + a) * P], ident_f[:])
+        nc.scalar.copy(out=v1T[:, 4 * P:6 * P], in_=tpb[:])
+        v1Tb = v1T[:].bitcast(BF16).rearrange("p (r e) -> p r e", e=2)
+
+        def gain_ap(i):
+            return g32[:, 16 * i:16 * i + 1]
 
         v2_k = v2_sb[:].rearrange("p c (b q e) -> p c b e q", b=4, e=2)
         w1g = const.tile([P, 2, D_H, 4], BF16, align_bytes=64)
@@ -90,16 +101,16 @@ def tile_feathernet_t_kernel(tc, x, V1, V2, w1_p, b1_p, w2_p, b2_p, out):
                         nc.tensor.matmul(
                             wp[:, j, :],
                             lhsT=v2_k[:, mc, 2 * g + u, e, :],
-                            rhs=v1T[:, mc, rc * P:(rc + 1) * P],
+                            rhs=v1Tb[:, rc * P:(rc + 1) * P, mc],
                             start=(mc == 0),
                             stop=(mc == 1),
                         )
                 dst = w1g[:, g, rc * P:(rc + 1) * P, :]
                 src = wp[:].rearrange("p j r -> p r j")
                 if rc % 2 == 0:
-                    nc.scalar.activation(out=dst, in_=src, func=ACT.Copy, scale=g32[:, 0:1])
+                    nc.scalar.activation(out=dst, in_=src, func=ACT.Copy, scale=gain_ap(0))
                 else:
-                    nc.vector.tensor_scalar(out=dst, in0=src, scalar1=g32[:, 0:1], scalar2=None, op0=ALU.mult)
+                    nc.vector.tensor_scalar(out=dst, in0=src, scalar1=gain_ap(0), scalar2=None, op0=ALU.mult)
             nc.vector.quantize_mx(
                 out=w1c[:, g * D_H:(g + 1) * D_H].bitcast(FP8X4),
                 scales=w1s[:, g * D_H:(g + 1) * D_H],
@@ -112,12 +123,12 @@ def tile_feathernet_t_kernel(tc, x, V1, V2, w1_p, b1_p, w2_p, b2_p, out):
                 nc.tensor.matmul(
                     bp[:, t, :],
                     lhsT=v2_sb[:, mc, t * P:(t + 1) * P],
-                    rhs=v1T[:, mc, 512:544],
+                    rhs=v1Tb[:, 512:544, mc],
                     start=(mc == 0),
                     stop=(mc == 1),
                 )
         b1_sb = const.tile([P, 4], F32)
-        nc.vector.tensor_scalar(out=b1_sb[:], in0=bp[:, :, 0], scalar1=g32[:, 1:2], scalar2=None, op0=ALU.mult)
+        nc.vector.tensor_scalar(out=b1_sb[:], in0=bp[:, :, 0], scalar1=gain_ap(1), scalar2=None, op0=ALU.mult)
 
         w2g = const.tile([P, P, 2, 4], BF16, align_bytes=64)
         w2c = const.tile([P, D_OUT], U32, align_bytes=64)
@@ -131,12 +142,12 @@ def tile_feathernet_t_kernel(tc, x, V1, V2, w1_p, b1_p, w2_p, b2_p, out):
                     nc.tensor.matmul(
                         wq[:, t, :],
                         lhsT=v2_sb[:, mc, col:col + P],
-                        rhs=v1T[:, mc, row:row + P],
+                        rhs=v1Tb[:, row:row + P, mc],
                         start=(mc == 0),
                         stop=(mc == 1),
                     )
             nc.scalar.activation(
-                out=w2g[:, :, par, :], in_=wq[:].rearrange("p t a -> p a t"), func=ACT.Copy, scale=g32[:, 2:3]
+                out=w2g[:, :, par, :], in_=wq[:].rearrange("p t a -> p a t"), func=ACT.Copy, scale=gain_ap(2)
             )
         nc.vector.quantize_mx(
             out=w2c[:].bitcast(FP8X4), scales=w2s[:], in_=w2g[:].rearrange("p a q t -> p (a q t)")
@@ -146,18 +157,18 @@ def tile_feathernet_t_kernel(tc, x, V1, V2, w1_p, b1_p, w2_p, b2_p, out):
         for mc in range(2):
             nc.tensor.matmul(
                 b2p[:],
-                lhsT=v1T[:, mc, 767:768].to_broadcast([P, P]),
+                lhsT=v1Tb[:, 767:768, mc].to_broadcast([P, P]),
                 rhs=v2_sb[:, mc, 512:768],
                 start=(mc == 0),
                 stop=(mc == 1),
             )
         b2bc = const.tile([P, 2, D_OUT], F32)
         for i in range(2):
-            nc.scalar.activation(out=b2bc[:, i, :], in_=b2p[:], func=ACT.Copy, scale=g32[:, 3:4])
+            nc.scalar.activation(out=b2bc[:, i, :], in_=b2p[:], func=ACT.Copy, scale=gain_ap(3))
 
-        xg, xc, xs, hb, hg, hc, hs, ysb = {}, {}, {}, {}, {}, {}, {}, {}
+        xg, xc, xs, hb, hg, hc, hs = {}, {}, {}, {}, {}, {}, {}
 
-        def transposes(c):
+        def transposes(c, on_vector):
             xw = x_sb[c][:].bitcast(F32).rearrange("p (s w) -> p s w", s=4)
             xg[c] = work.tile([P, 4 * D_IN], BF16, align_bytes=64, name="xg")
             xgf = xg[c][:].bitcast(F32).rearrange("p (g n u) -> p g n u", g=2, u=2)
@@ -172,20 +183,19 @@ def tile_feathernet_t_kernel(tc, x, V1, V2, w1_p, b1_p, w2_p, b2_p, out):
                             )
                     dst = xgf[:, g, 256 * sp:256 * (sp + 1), :]
                     src = xt[:].rearrange("p u n -> p n u")
-                    if c <= LEAD and sp == 1:
+                    if on_vector[2 * g + sp]:
                         nc.vector.tensor_copy(out=dst, in_=src)
                     else:
                         nc.scalar.copy(out=dst, in_=src)
-
-        def quant_x(c):
             xc[c] = xq.tile([P, 2 * CH], U32, align_bytes=64, name="xc")
             xs[c] = xq.tile([P, 2 * CH], U8, align_bytes=64, name="xs")
-            for g in range(2):
-                nc.vector.quantize_mx(
-                    out=xc[c][:, g * CH:(g + 1) * CH].bitcast(FP8X4),
-                    scales=xs[c][:, g * CH:(g + 1) * CH],
-                    in_=xg[c][:, g * 4 * CH:(g + 1) * 4 * CH],
-                )
+
+        def quant_x(c, g):
+            nc.vector.quantize_mx(
+                out=xc[c][:, g * CH:(g + 1) * CH].bitcast(FP8X4),
+                scales=xs[c][:, g * CH:(g + 1) * CH],
+                in_=xg[c][:, g * 4 * CH:(g + 1) * 4 * CH],
+            )
 
         def layer1(c):
             hb[c] = work.tile([P, 4, CH], BF16, name="hb")
@@ -202,45 +212,37 @@ def tile_feathernet_t_kernel(tc, x, V1, V2, w1_p, b1_p, w2_p, b2_p, out):
                         start=(g == 0),
                         stop=(g == 1),
                     )
-                if t == V_H_BANK:
-                    nc.vector.tensor_scalar(
-                        out=hb[c][:, t, :], in0=hp[:], scalar1=b1_sb[:, t:t + 1], scalar2=0.0, op0=ALU.add, op1=ALU.max
+                nc.scalar.activation(out=hb[c][:, t, :], in_=hp[:], func=ACT.Relu, bias=b1_sb[:, t:t + 1], scale=1.0)
+
+        def regroup_h(c, engines):
+            hg[c] = work.tile([P, CH, 4], BF16, align_bytes=64, name="hg")
+            hc[c] = hq.tile([P, CH], U32, align_bytes=64, name="hc")
+            hs[c] = hq.tile([P, CH], U8, align_bytes=64, name="hs")
+            for half in (1, 0):
+                n0 = half * HALF
+                dst = hg[c][:, n0:n0 + HALF, :]
+                src = hb[c][:, :, n0:n0 + HALF]
+                if engines[half] == "g":
+                    nc.gpsimd.tensor_scalar(
+                        out=dst, in0=src.rearrange("p t n -> p n t"), scalar1=1.0, scalar2=0.0, op0=ALU.mult, op1=ALU.add
                     )
+                elif engines[half] == "s":
+                    nc.scalar.copy(out=dst, in_=src.rearrange("p t n -> p n t"))
                 else:
-                    nc.scalar.activation(
-                        out=hb[c][:, t, :], in_=hp[:], func=ACT.Relu, bias=b1_sb[:, t:t + 1], scale=1.0
+                    nc.vector.tensor_copy(
+                        out=dst.rearrange("p (c i) t -> p c t i", i=4), in_=src.rearrange("p t (c i) -> p c t i", i=4)
                     )
 
-        def regroup_h(c):
-            hg[c] = work.tile([P, CH, 4], BF16, align_bytes=64, name="hg")
-            v_tok = CH - G_TOK
-            if G_TOK > 0:
-                nc.gpsimd.tensor_scalar(
-                    out=hg[c][:, v_tok:CH, :],
-                    in0=hb[c][:, :, v_tok:CH].rearrange("p t n -> p n t"),
-                    scalar1=1.0,
-                    scalar2=0.0,
-                    op0=ALU.mult,
-                    op1=ALU.add,
-                )
-            nc.vector.tensor_copy(
-                out=hg[c][:, 0:v_tok, :].rearrange("p (c i) t -> p c t i", i=4),
-                in_=hb[c][:, :, 0:v_tok].rearrange("p t (c i) -> p c t i", i=4),
+        def quant_h(c, half):
+            n0 = half * HALF
+            nc.vector.quantize_mx(
+                out=hc[c][:, n0:n0 + HALF].bitcast(FP8X4),
+                scales=hs[c][:, n0:n0 + HALF],
+                in_=hg[c][:, n0:n0 + HALF, :].rearrange("p n t -> p (n t)"),
             )
 
-        def quant_h(c):
-            hc[c] = work.tile([P, CH], U32, align_bytes=64, name="hc")
-            hs[c] = work.tile([P, CH], U8, align_bytes=64, name="hs")
-            for half in range(2):
-                n0 = half * 256
-                nc.vector.quantize_mx(
-                    out=hc[c][:, n0:n0 + 256].bitcast(FP8X4),
-                    scales=hs[c][:, n0:n0 + 256],
-                    in_=hg[c][:, n0:n0 + 256, :].rearrange("p n t -> p (n t)"),
-                )
-
         def layer2(c):
-            ysb[c] = ypool.tile([P, 4, D_OUT], F32, name="ysb")
+            ysb = ypool.tile([P, 4, D_OUT], F32, name="ysb")
             for half in range(2):
                 yp = psum.tile([P, 2, D_OUT], F32, tag="ps", name="yp")
                 for s2 in range(2):
@@ -254,21 +256,38 @@ def tile_feathernet_t_kernel(tc, x, V1, V2, w1_p, b1_p, w2_p, b2_p, out):
                         start=True,
                         stop=True,
                     )
-                nc.vector.tensor_tensor(out=ysb[c][:, 2 * half:2 * half + 2, :], in0=yp[:], in1=b2bc[:], op=ALU.add)
-            nc.sync.dma_start(out=out[c * CH:(c + 1) * CH, :].rearrange("(p s) o -> p s o", s=4), in_=ysb[c][:])
+                nc.vector.tensor_tensor(out=ysb[:, 2 * half:2 * half + 2, :], in0=yp[:], in1=b2bc[:], op=ALU.add)
+            nc.sync.dma_start(out=out[c * CH:(c + 1) * CH, :].rearrange("(p s) o -> p s o", s=4), in_=ysb[:])
 
+        shared = (0, 1, 0, 1)
         for c in range(LEAD):
-            transposes(c)
-            quant_x(c)
+            transposes(c, shared)
+            quant_x(c, 0)
+            quant_x(c, 1)
+        next_l2 = 0
         for c in range(NCH + 1):
-            if c + LEAD < NCH:
-                transposes(c + LEAD)
-            if c >= 1:
-                regroup_h(c - 1)
-                quant_h(c - 1)
-            if c + LEAD < NCH:
-                quant_x(c + LEAD)
+            cx, ch = c + LEAD, c - 1
+            more_x = cx < NCH
+            if more_x:
+                transposes(cx, shared if c == 0 else (X_ON_V[c % len(X_ON_V)], 0, 0, 0))
+            if ch >= 0:
+                if more_x:
+                    regroup_h(ch, ("v", "g"))
+                elif ch < NCH - 1:
+                    regroup_h(ch, ("s", "g"))
+                else:
+                    regroup_h(ch, ("s", "v"))
+            if more_x:
+                quant_x(cx, 0)
+            if ch >= 0:
+                quant_h(ch, 0 if ch < NCH - 1 else 1)
+            if more_x:
+                quant_x(cx, 1)
+            if ch >= 0:
+                quant_h(ch, 1 if ch < NCH - 1 else 0)
             if c < NCH:
                 layer1(c)
-            if c >= 1:
-                layer2(c - 1)
+            last_l2 = c - LAG if more_x else c - 1
+            for cy in range(next_l2, last_l2 + 1):
+                layer2(cy)
+            next_l2 = max(next_l2, last_l2 + 1)

from contextlib import ExitStack

import concourse.mybir as mybir
from concourse.masks import make_identity

F32 = mybir.dt.float32
BF16 = mybir.dt.bfloat16
U32 = mybir.dt.uint32
U8 = mybir.dt.uint8
FP8X4 = mybir.dt.float8_e4m3fn_x4
ACT = mybir.ActivationFunctionType
ALU = mybir.AluOpType

P = 128
B, D_IN, D_H, D_OUT = 8192, 1024, 512, 256
RANK = 256
CH = 512
HALF = CH // 2
NCH = B // CH
LEAD = 2
LAG = 2
X_ON_V = (1, 0, 0)
WARM_A, WARM_B = 4, 2
FLOPS = 2 * B * D_IN * D_H + 2 * B * D_H * D_OUT + 2 * 1024 * RANK * 1024


def tile_feathernet_t_kernel(tc, x, V1, V2, w1_p, b1_p, w2_p, b2_p, out):
    nc = tc.nc
    with ExitStack() as ctx:
        ctx.enter_context(tc.manual_schedule())
        const = ctx.enter_context(tc.tile_pool(name="const", bufs=1))
        xin = ctx.enter_context(tc.tile_pool(name="xin", bufs=NCH))
        work = ctx.enter_context(tc.tile_pool(name="work", bufs=2))
        xq = ctx.enter_context(tc.tile_pool(name="xq", bufs=LEAD + 1))
        hq = ctx.enter_context(tc.tile_pool(name="hq", bufs=LAG + 1))
        ypool = ctx.enter_context(tc.tile_pool(name="ypool", bufs=4))
        psum = ctx.enter_context(tc.psum_pool(name="psum", bufs=8))

        ones = const.tile([P, CH], BF16)
        nc.vector.memset(ones[:], 1.0)
        gain_row = const.tile([P, 64], BF16)
        nc.vector.memset(gain_row[:], 0.0)
        ident_f = const.tile([P, P], F32)
        make_identity(nc, ident_f[:])

        v1_sb = const.tile([P, 6, RANK], BF16)
        v2_sb = const.tile([P, 2, 1024], BF16)
        nc.sync.dma_start(out=v1_sb[:, 0:4, :], in_=V1[0:512, :].rearrange("(a p) m -> p a m", p=P))
        nc.sync.dma_start(out=v2_sb[:], in_=V2.rearrange("(q e) n -> q e n", e=2))
        nc.sync.dma_start(out=v1_sb[:, 4, :], in_=V1[512:640, :])
        nc.sync.dma_start(out=v1_sb[:, 5, :], in_=V1[513:641, :])
        for i, gain in enumerate((w1_p, b1_p, w2_p, b2_p)):
            nc.scalar.dma_start(out=gain_row[0:1, 16 * i:16 * i + 1], in_=gain.rearrange("(o n) -> o n", o=1))
        x_sb = []
        for c in range(NCH):
            xt_in = xin.tile([P, 4 * D_IN], BF16, name="x_sb")
            nc.sync.dma_start(
                out=xt_in[:],
                in_=x[c * CH:(c + 1) * CH, :].rearrange("(p s) k -> p (s k)", s=4),
            )
            x_sb.append(xt_in)

        warm = psum.tile([P, CH], F32, tag="ps", name="warm")

        def dummies(n):
            for i in range(n):
                nc.tensor.matmul(warm[:], lhsT=ones[:, 0:P], rhs=ones[:], start=True, stop=True)

        dummies(WARM_A)

        v1w = v1_sb[:].rearrange("p a m -> p (a m)").bitcast(F32)
        v1T = const.tile([P, 6 * P], F32)
        tpa = psum.tile([P, 4 * P], F32, tag="ps", name="tpa")
        for a in range(4):
            nc.tensor.transpose(tpa[:, a * P:(a + 1) * P], v1w[:, a * P:(a + 1) * P], ident_f[:])
        nc.vector.tensor_copy(out=v1T[:, 0:4 * P], in_=tpa[:])
        gp = psum.tile([P, 64], F32, tag="ps", name="gp")
        nc.tensor.matmul(gp[:], lhsT=ones[:, 0:P], rhs=gain_row[:], start=True, stop=True)
        g32 = const.tile([P, 64], F32)
        nc.vector.tensor_copy(out=g32[:], in_=gp[:])
        dummies(WARM_B)
        tpb = psum.tile([P, 2 * P], F32, tag="ps", name="tpb")
        for a in range(2):
            nc.tensor.transpose(tpb[:, a * P:(a + 1) * P], v1w[:, (4 + a) * P:(5 + a) * P], ident_f[:])
        nc.scalar.copy(out=v1T[:, 4 * P:6 * P], in_=tpb[:])
        v1Tb = v1T[:].bitcast(BF16).rearrange("p (r e) -> p r e", e=2)

        def gain_ap(i):
            return g32[:, 16 * i:16 * i + 1]

        v2_k = v2_sb[:].rearrange("p c (b q e) -> p c b e q", b=4, e=2)
        w1g = const.tile([P, 2, D_H, 4], BF16, align_bytes=64)
        w1c = const.tile([P, 2 * D_H], U32, align_bytes=64)
        w1s = const.tile([P, 2 * D_H], U8, align_bytes=64)
        for g in range(2):
            for rc in range(4):
                wp = psum.tile([P, 4, P], F32, tag="ps", name="wp")
                for j in range(4):
                    u, e = j // 2, j % 2
                    for mc in range(2):
                        nc.tensor.matmul(
                            wp[:, j, :],
                            lhsT=v2_k[:, mc, 2 * g + u, e, :],
                            rhs=v1Tb[:, rc * P:(rc + 1) * P, mc],
                            start=(mc == 0),
                            stop=(mc == 1),
                        )
                dst = w1g[:, g, rc * P:(rc + 1) * P, :]
                src = wp[:].rearrange("p j r -> p r j")
                if rc % 2 == 0:
                    nc.scalar.activation(out=dst, in_=src, func=ACT.Copy, scale=gain_ap(0))
                else:
                    nc.vector.tensor_scalar(out=dst, in0=src, scalar1=gain_ap(0), scalar2=None, op0=ALU.mult)
            nc.vector.quantize_mx(
                out=w1c[:, g * D_H:(g + 1) * D_H].bitcast(FP8X4),
                scales=w1s[:, g * D_H:(g + 1) * D_H],
                in_=w1g[:, g, :, :].rearrange("p r j -> p (r j)"),
            )

        bp = psum.tile([P, 4, 32], F32, tag="ps", name="bp")
        for t in range(4):
            for mc in range(2):
                nc.tensor.matmul(
                    bp[:, t, :],
                    lhsT=v2_sb[:, mc, t * P:(t + 1) * P],
                    rhs=v1Tb[:, 512:544, mc],
                    start=(mc == 0),
                    stop=(mc == 1),
                )
        b1_sb = const.tile([P, 4], F32)
        nc.vector.tensor_scalar(out=b1_sb[:], in0=bp[:, :, 0], scalar1=gain_ap(1), scalar2=None, op0=ALU.mult)

        w2g = const.tile([P, P, 2, 4], BF16, align_bytes=64)
        w2c = const.tile([P, D_OUT], U32, align_bytes=64)
        w2s = const.tile([P, D_OUT], U8, align_bytes=64)
        for par in range(2):
            wq = psum.tile([P, 4, P], F32, tag="ps", name="wq")
            for t in range(4):
                col = t * P + (512 if par == 0 else 0)
                row = 512 if par == 0 else 640
                for mc in range(2):
                    nc.tensor.matmul(
                        wq[:, t, :],
                        lhsT=v2_sb[:, mc, col:col + P],
                        rhs=v1Tb[:, row:row + P, mc],
                        start=(mc == 0),
                        stop=(mc == 1),
                    )
            nc.scalar.activation(
                out=w2g[:, :, par, :], in_=wq[:].rearrange("p t a -> p a t"), func=ACT.Copy, scale=gain_ap(2)
            )
        nc.vector.quantize_mx(
            out=w2c[:].bitcast(FP8X4), scales=w2s[:], in_=w2g[:].rearrange("p a q t -> p (a q t)")
        )

        b2p = psum.tile([P, D_OUT], F32, tag="ps", name="b2p")
        for mc in range(2):
            nc.tensor.matmul(
                b2p[:],
                lhsT=v1Tb[:, 767:768, mc].to_broadcast([P, P]),
                rhs=v2_sb[:, mc, 512:768],
                start=(mc == 0),
                stop=(mc == 1),
            )
        b2bc = const.tile([P, 2, D_OUT], F32)
        for i in range(2):
            nc.scalar.activation(out=b2bc[:, i, :], in_=b2p[:], func=ACT.Copy, scale=gain_ap(3))

        xg, xc, xs, hb, hg, hc, hs = {}, {}, {}, {}, {}, {}, {}

        def transposes(c, on_vector):
            xw = x_sb[c][:].bitcast(F32).rearrange("p (s w) -> p s w", s=4)
            xg[c] = work.tile([P, 4 * D_IN], BF16, align_bytes=64, name="xg")
            xgf = xg[c][:].bitcast(F32).rearrange("p (g n u) -> p g n u", g=2, u=2)
            for g in range(2):
                for sp in range(2):
                    xt = psum.tile([P, 2, 2 * P], F32, tag="ps", name="xt")
                    for s2 in range(2):
                        for u in range(2):
                            w0 = 256 * g + 128 * u
                            nc.tensor.transpose(
                                xt[:, u, s2 * P:(s2 + 1) * P], xw[:, 2 * sp + s2, w0:w0 + P], ident_f[:]
                            )
                    dst = xgf[:, g, 256 * sp:256 * (sp + 1), :]
                    src = xt[:].rearrange("p u n -> p n u")
                    if on_vector[2 * g + sp]:
                        nc.vector.tensor_copy(out=dst, in_=src)
                    else:
                        nc.scalar.copy(out=dst, in_=src)
            xc[c] = xq.tile([P, 2 * CH], U32, align_bytes=64, name="xc")
            xs[c] = xq.tile([P, 2 * CH], U8, align_bytes=64, name="xs")

        def quant_x(c, g):
            nc.vector.quantize_mx(
                out=xc[c][:, g * CH:(g + 1) * CH].bitcast(FP8X4),
                scales=xs[c][:, g * CH:(g + 1) * CH],
                in_=xg[c][:, g * 4 * CH:(g + 1) * 4 * CH],
            )

        def layer1(c):
            hb[c] = work.tile([P, 4, CH], BF16, name="hb")
            for t in range(4):
                hp = psum.tile([P, CH], F32, tag="ps", name="hp")
                for g in range(2):
                    k0 = g * D_H + t * P
                    nc.tensor.matmul_mx(
                        out=hp[:],
                        lhsT=w1c[:, k0:k0 + P].bitcast(FP8X4),
                        lhsT_scale=w1s[:, k0:k0 + P],
                        rhs=xc[c][:, g * CH:(g + 1) * CH].bitcast(FP8X4),
                        rhs_scale=xs[c][:, g * CH:(g + 1) * CH],
                        start=(g == 0),
                        stop=(g == 1),
                    )
                nc.scalar.activation(out=hb[c][:, t, :], in_=hp[:], func=ACT.Relu, bias=b1_sb[:, t:t + 1], scale=1.0)

        def regroup_h(c, engines):
            hg[c] = work.tile([P, CH, 4], BF16, align_bytes=64, name="hg")
            hc[c] = hq.tile([P, CH], U32, align_bytes=64, name="hc")
            hs[c] = hq.tile([P, CH], U8, align_bytes=64, name="hs")
            for half in (1, 0):
                n0 = half * HALF
                dst = hg[c][:, n0:n0 + HALF, :]
                src = hb[c][:, :, n0:n0 + HALF]
                if engines[half] == "g":
                    nc.gpsimd.tensor_scalar(
                        out=dst, in0=src.rearrange("p t n -> p n t"), scalar1=1.0, scalar2=0.0, op0=ALU.mult, op1=ALU.add
                    )
                elif engines[half] == "s":
                    nc.scalar.copy(out=dst, in_=src.rearrange("p t n -> p n t"))
                else:
                    nc.vector.tensor_copy(
                        out=dst.rearrange("p (c i) t -> p c t i", i=4), in_=src.rearrange("p t (c i) -> p c t i", i=4)
                    )

        def quant_h(c, half):
            n0 = half * HALF
            nc.vector.quantize_mx(
                out=hc[c][:, n0:n0 + HALF].bitcast(FP8X4),
                scales=hs[c][:, n0:n0 + HALF],
                in_=hg[c][:, n0:n0 + HALF, :].rearrange("p n t -> p (n t)"),
            )

        def layer2(c):
            ysb = ypool.tile([P, 4, D_OUT], F32, name="ysb")
            for half in range(2):
                yp = psum.tile([P, 2, D_OUT], F32, tag="ps", name="yp")
                for s2 in range(2):
                    s = 2 * half + s2
                    nc.tensor.matmul_mx(
                        out=yp[:, s2, :],
                        lhsT=hc[c][:, s * P:(s + 1) * P].bitcast(FP8X4),
                        lhsT_scale=hs[c][:, s * P:(s + 1) * P],
                        rhs=w2c[:].bitcast(FP8X4),
                        rhs_scale=w2s[:],
                        start=True,
                        stop=True,
                    )
                nc.vector.tensor_tensor(out=ysb[:, 2 * half:2 * half + 2, :], in0=yp[:], in1=b2bc[:], op=ALU.add)
            nc.sync.dma_start(out=out[c * CH:(c + 1) * CH, :].rearrange("(p s) o -> p s o", s=4), in_=ysb[:])

        shared = (0, 1, 0, 1)
        for c in range(LEAD):
            transposes(c, shared)
            quant_x(c, 0)
            quant_x(c, 1)
        next_l2 = 0
        for c in range(NCH + 1):
            cx, ch = c + LEAD, c - 1
            more_x = cx < NCH
            if more_x:
                transposes(cx, shared if c == 0 else (X_ON_V[c % len(X_ON_V)], 0, 0, 0))
            if ch >= 0:
                if more_x:
                    regroup_h(ch, ("v", "g"))
                elif ch < NCH - 1:
                    regroup_h(ch, ("s", "g"))
                else:
                    regroup_h(ch, ("s", "v"))
            if more_x:
                quant_x(cx, 0)
            if ch >= 0:
                quant_h(ch, 0 if ch < NCH - 1 else 1)
            if more_x:
                quant_x(cx, 1)
            if ch >= 0:
                quant_h(ch, 1 if ch < NCH - 1 else 0)
            if c < NCH:
                layer1(c)
            last_l2 = c - LAG if more_x else c - 1
            for cy in range(next_l2, last_l2 + 1):
                layer2(cy)
            next_l2 = max(next_l2, last_l2 + 1)
